import numpy as np
import ml_dtypes


def mxq(x, axis, fmt="e4m3"):
    dtype, down = {"e4m3": (ml_dtypes.float8_e4m3fn, 7), "e5m2": (ml_dtypes.float8_e5m2, 14)}[fmt]
    v = np.moveaxis(np.asarray(x, np.float32).astype(ml_dtypes.bfloat16).astype(np.float64), axis, -1)
    blocks = v.reshape(v.shape[:-1] + (-1, 32))
    amax = np.abs(blocks).max(-1, keepdims=True)
    byte = np.maximum(np.where(amax > 0, np.frexp(amax)[1] - 1 + 127, 0) - down, 1)
    scale = np.exp2(byte - 127.0)
    codes = (blocks / scale).astype(np.float32).astype(dtype).astype(np.float64)
    return np.moveaxis((codes * scale).reshape(v.shape), -1, axis)


WIDE = False


def mx_kscale(k):
    if not WIDE:
        return np.ones(k)
    levels = np.array([10, -10, 5, -5, 0])
    a = np.random.permutation(np.resize(levels, k // 512 * 4)).reshape(k // 512, 4)
    idx = np.arange(k)
    return np.exp2(a[idx // 512, idx % 128 // 32])


BF16 = ml_dtypes.bfloat16


def bf(x):
    return np.asarray(x, np.float32).astype(BF16)


def f64(x):
    return np.asarray(x).astype(np.float64)


E2M1 = np.array([0.0, 0.5, 1.0, 1.5, 2.0, 3.0, 4.0, 6.0, -0.0, -0.5, -1.0, -1.5, -2.0, -3.0, -4.0, -6.0])


def pack_weight(w, fmt):
    k, n = w.shape
    w = f64(bf(w)).reshape(k // 32, 32, n)
    amax = np.abs(w).max(1)
    if fmt == "e4m3":
        byte = np.frexp(amax)[1] - 1 + 127 - 7
    else:
        mant, ex = np.frexp(amax / 6.0)
        byte = np.where(mant > 0.5, ex, ex - 1) + 127
    byte = np.clip(np.where(amax > 0, byte, 1), 1, 254)
    scaled = (w * np.exp2(127.0 - byte)[:, None, :]).reshape(k, n).astype(np.float32)
    by_word = np.ascontiguousarray(scaled.reshape(k // 512, 128, 4, n).transpose(0, 1, 3, 2))
    if fmt == "e4m3":
        words = by_word.astype(ml_dtypes.float8_e4m3fn).view(np.uint8)
    else:
        c = by_word.astype(ml_dtypes.float4_e2m1fn).view(np.uint8) & 0xF
        words = c[..., 0::2] | (c[..., 1::2] << 4)
    return np.ascontiguousarray(words), np.ascontiguousarray(byte.astype(np.uint8).reshape(k // 512, 16, n))


def unpack_weight(words, scales, fmt):
    g, p, n, _ = words.shape
    if fmt == "e4m3":
        vals = np.ascontiguousarray(words).view(ml_dtypes.float8_e4m3fn).astype(np.float64)
    else:
        nib = np.empty((g, p, n, 4), np.uint8)
        nib[..., 0::2] = words & 0xF
        nib[..., 1::2] = words >> 4
        vals = E2M1[nib]
    vals = vals * np.repeat(np.exp2(scales.astype(np.float64) - 127.0), 8, axis=1)[..., None]
    return vals.transpose(0, 1, 3, 2).reshape(g * 512, n)


E, F, H, MID, OUT = 128, 256, 768, 4096, 2048
D = 2 * (F + H)
IN = D + 1
FMT = "e4m3"


def setup_inputs():
    s = mx_kscale(D)
    t = mx_kscale(MID)
    w1 = np.concatenate([np.random.standard_normal((MID, D)) / np.sqrt(D) / s[None, :],
                         np.random.standard_normal((MID, 1)) * 0.5], axis=1) * t[:, None]
    dst_node_feat = bf(np.random.standard_normal((E, F)) * s[:F])
    dst_node_hidden = bf(np.random.standard_normal((E, H)) * s[F:F + H])
    src_node_feat = bf(np.random.standard_normal((E, F)) * s[F + H:2 * F + H])
    src_node_hidden = bf(np.random.standard_normal((E, H)) * s[2 * F + H:])
    edge_feat = bf(np.random.standard_normal(E))
    b1 = bf(np.random.standard_normal(MID) * 0.3 * t)
    w2 = np.random.standard_normal((OUT, MID)) / np.sqrt(MID) / t[None, :]
    w2_words, w2_scales = pack_weight(np.ascontiguousarray(w2.T), FMT)
    b2 = bf(np.random.standard_normal(OUT) * 0.3)
    return {"dst_node_feat": dst_node_feat,
            "dst_node_hidden": dst_node_hidden,
            "src_node_feat": src_node_feat,
            "src_node_hidden": src_node_hidden,
            "edge_feat": edge_feat,
            "W1": bf(w1),
            "b1": b1,
            "W2_words": w2_words,
            "W2_scales": w2_scales,
            "b2": b2}


def reference(dst_node_feat, dst_node_hidden, src_node_feat, src_node_hidden, edge_feat, W1, b1, W2_words, W2_scales, b2):
    x = np.concatenate([f64(dst_node_feat), f64(dst_node_hidden), f64(src_node_feat), f64(src_node_hidden),
                        f64(edge_feat)[:, None]], axis=1)
    w1 = f64(W1)
    pre = (mxq(x[:, :D], 1, "e4m3") @ mxq(w1[:, :D], 1, "e4m3").T) + x[:, D:] * w1[:, D] + f64(b1)
    h = np.maximum(pre, 0.0)
    return np.tanh((mxq(h, 1, "e4m3") @ unpack_weight(W2_words, W2_scales, FMT)) + f64(b2))

@@ -1,0 +1,307 @@
+from contextlib import ExitStack
+
+import concourse.mybir as mybir
+from concourse.masks import make_identity
+
+F32 = mybir.dt.float32
+BF16 = mybir.dt.bfloat16
+I32 = mybir.dt.int32
+U32 = mybir.dt.uint32
+U8 = mybir.dt.uint8
+FP8X4 = mybir.dt.float8_e4m3fn_x4
+ADD = mybir.AluOpType.add
+MULT = mybir.AluOpType.mult
+ACT = mybir.ActivationFunctionType
+
+P = 128
+E = 128
+D = 2048
+MID = 4096
+OUT = 2048
+G = MID // 512
+UNITS = 2 * G
+ROW_PITCH = 2064
+SLOTS = 14
+
+FLOPS = 2 * E * (D + 1) * MID + 2 * E * MID * OUT
+
+
+def tile_edgenetwork_w_kernel(
+    tc,
+    dst_node_feat,
+    dst_node_hidden,
+    src_node_feat,
+    src_node_hidden,
+    edge_feat,
+    W1,
+    b1,
+    W2_words,
+    W2_scales,
+    b2,
+    out,
+):
+    nc = tc.nc
+    with ExitStack() as ctx:
+        ctx.enter_context(tc.manual_schedule())
+        const = ctx.enter_context(tc.tile_pool(name="const", bufs=1))
+        big = ctx.enter_context(tc.tile_pool(name="big", bufs=SLOTS))
+        work = ctx.enter_context(tc.tile_pool(name="work", bufs=3))
+        small = ctx.enter_context(tc.tile_pool(name="small", bufs=2))
+        fin = ctx.enter_context(tc.tile_pool(name="fin", bufs=4))
+        psum = ctx.enter_context(tc.psum_pool(name="psum", bufs=6))
+
+        w1_view = W1.rearrange("(g p j) k -> g p j k", g=G, p=P, j=4)
+
+        raw = {}
+        banks = {}
+        grouped = {}
+        codes = {}
+        planes1 = {}
+        hidden = {}
+        addend = {}
+        pre = {}
+        h_grouped = {}
+        w2_tiles = {}
+
+        def load_unit(s):
+            r = big.tile([P, 2, ROW_PITCH], BF16, name="raw", tag="big", align_bytes=64)
+            g, jh = s // 2, s % 2
+            nc.sync.dma_start(out=r[:, :, 0 : D + 1], in_=w1_view[g][:, 2 * jh : 2 * jh + 2, :])
+            raw[s] = r
+
+        def load_w2(g):
+            w = big.tile([P, OUT], U32, name="w2", tag="big", align_bytes=64)
+            src = W2_words[g].rearrange("p n t -> p (n t)").bitcast(I32)
+            if g < G - 1:
+                nc.sync.dma_start(out=w[:].bitcast(I32), in_=src)
+            else:
+                for nq in range(4):
+                    cols = slice(nq * 512, (nq + 1) * 512)
+                    nc.sync.dma_start(out=w[:, cols].bitcast(I32), in_=src[:, cols])
+            w2_tiles[g] = w
+
+        ident = const.tile([P, P], F32, name="ident")
+        make_identity(nc, ident[:])
+        warm_in = const.tile([P, 1], F32, name="warm_in")
+        warm_out = const.tile([P, 1], F32, name="warm_out")
+        nc.vector.memset(warm_in[:], 0.0)
+        nc.scalar.activation(out=warm_out[:], in_=warm_in[:], func=ACT.Tanh)
+
+        b1_rows = const.tile([P, 512], BF16, name="b1_rows")
+        nc.vector.memset(b1_rows[:].bitcast(I32), 0)
+        row = const.tile([P, OUT + E], BF16, name="row")
+        nc.vector.memset(row[:].bitcast(I32), 0)
+        ones = const.tile([P, P], BF16, name="ones")
+        nc.vector.memset(ones[:], 1.0)
+        w2_planes = const.tile([P, 2, OUT], U8, name="w2_planes", align_bytes=64)
+        nc.vector.memset(w2_planes[:].bitcast(I32), 0)
+
+        load_unit(0)
+        nc.scalar.dma_start(out=b1_rows[0:G, :], in_=b1.rearrange("(g c) -> g c", g=G))
+        nc.scalar.dma_start(out=row[0:1, OUT : OUT + E], in_=edge_feat.rearrange("(o n) -> o n", o=1))
+        nc.scalar.dma_start(out=row[0:1, 0:OUT], in_=b2.rearrange("(o n) -> o n", o=1))
+
+        x_raw = const.tile([P, D], BF16, name="x_raw")
+        nc.sync.dma_start(out=x_raw[:, 0:256], in_=dst_node_feat)
+        nc.sync.dma_start(out=x_raw[:, 256:1024], in_=dst_node_hidden)
+        nc.sync.dma_start(out=x_raw[:, 1024:1280], in_=src_node_feat)
+        nc.sync.dma_start(out=x_raw[:, 1280:2048], in_=src_node_hidden)
+        for s in range(1, SLOTS):
+            load_unit(s)
+
+        b1_f32 = const.tile([P, 4, P], F32, name="b1_f32")
+        nc.vector.tensor_copy(out=b1_f32[:], in_=b1_rows[:].rearrange("r (p j) -> r j p", j=4))
+
+        w1_edge = const.tile([P, G, 4], F32, name="w1_edge")
+        b1_col = const.tile([P, G, 4], F32, name="b1_col")
+        edge_all = const.tile([P, E], F32, name="edge_all")
+        b2_all = const.tile([P, OUT], F32, name="b2_all")
+        x_grouped = const.tile([P, D], BF16, name="x_grouped", align_bytes=64)
+        x_codes = const.tile([P, D // 4], U32, name="x_codes", align_bytes=64)
+        x_planes = const.tile([P, D // 4], U8, name="x_planes", align_bytes=64)
+        h_codes = const.tile([P, G, E], U32, name="h_codes", align_bytes=64)
+        h_planes = const.tile([P, G, E], U8, name="h_planes", align_bytes=64)
+
+        def transpose_words(src_words, first_pass):
+            bank = psum.tile([P, 512], F32, name="tp", tag="tp")
+            for cc in range(2):
+                for u in range(2):
+                    col = 256 * (first_pass + cc) + 128 * u
+                    nc.tensor.transpose(
+                        bank[:, (2 * cc + u) * P : (2 * cc + u + 1) * P],
+                        src_words[:, col : col + P],
+                        ident[:],
+                    )
+            return bank
+
+        def copy_out(engine_is_vector, dst_words, bank):
+            src = bank[:].rearrange("w (c u p) -> w c p u", c=2, u=2, p=P)
+            if engine_is_vector:
+                nc.vector.tensor_copy(out=dst_words, in_=src)
+            else:
+                nc.scalar.copy(out=dst_words, in_=src)
+
+        def transposes(s):
+            banks[s] = [
+                transpose_words(raw[s][:, b // 2, 0:D].bitcast(F32), 2 * (b % 2)) for b in range(4)
+            ]
+
+        def edge_column(s):
+            g, jh = s // 2, s % 2
+            nc.vector.tensor_copy(out=w1_edge[:, g, 2 * jh : 2 * jh + 2], in_=raw[s][:, :, D])
+
+        def scalar_copies(s):
+            gr = work.tile([P, 4096], BF16, name="grouped", tag="grouped", align_bytes=64)
+            grouped[s] = gr
+            words = gr[:].bitcast(F32).rearrange("w (o p u) -> w o p u", o=8, p=P, u=2)
+            last = 3 if s % 2 == 0 else 4
+            for b in range(last):
+                copy_out(False, words[:, 2 * b : 2 * b + 2], banks[s][b])
+
+        def vector_copies(s):
+            if s % 2 == 0:
+                words = grouped[s][:].bitcast(F32).rearrange("w (o p u) -> w o p u", o=8, p=P, u=2)
+                copy_out(True, words[:, 6:8], banks[s][3])
+
+        def quantise(s):
+            c = work.tile([P, 1024], U32, name="codes", tag="codes", align_bytes=64)
+            pl = work.tile([P, 1024], U8, name="planes", tag="planes", align_bytes=64)
+            nc.vector.quantize_mx(out=c[:].bitcast(FP8X4), scales=pl[:], in_=grouped[s][:])
+            codes[s] = c
+            planes1[s] = pl
+
+        def layer1(s):
+            g, jh = s // 2, s % 2
+            if jh == 0:
+                hidden[g] = psum.tile([P, 512], F32, name="hp", tag="hp", bufs=2)
+            for jj in range(2):
+                j = 2 * jh + jj
+                for c in range(4):
+                    o = 4 * jj + c
+                    nc.tensor.matmul_mx(
+                        out=hidden[g][:, j * E : (j + 1) * E],
+                        lhsT=codes[s][:, o * P : (o + 1) * P].bitcast(FP8X4),
+                        lhsT_scale=planes1[s][:, o * P : (o + 1) * P],
+                        rhs=x_codes[:, c * E : (c + 1) * E].bitcast(FP8X4),
+                        rhs_scale=x_planes[:, c * E : (c + 1) * E],
+                        start=(c == 0),
+                        stop=(c == 3),
+                    )
+
+        def make_addend(g):
+            a = small.tile([P, 4, E], F32, name="addend", tag="addend")
+            for j in range(4):
+                nc.vector.tensor_scalar(
+                    out=a[:, j, :],
+                    in0=edge_all[:],
+                    scalar1=w1_edge[:, g, j : j + 1],
+                    scalar2=b1_col[:, g, j : j + 1],
+                    op0=MULT,
+                    op1=ADD,
+                )
+            addend[g] = a
+
+        def add_terms(g):
+            z = small.tile([P, E, 4], F32, name="pre", tag="pre")
+            nc.vector.tensor_tensor(
+                out=z[:],
+                in0=hidden[g][:].rearrange("p (j e) -> p e j", j=4),
+                in1=addend[g][:].rearrange("p j e -> p e j"),
+                op=ADD,
+            )
+            pre[g] = z
+
+        def relu(g):
+            hg = small.tile([P, 4 * E], BF16, name="h_grouped", tag="h_grouped", align_bytes=64)
+            nc.scalar.activation(out=hg[:], in_=pre[g][:].rearrange("p e j -> p (e j)"), func=ACT.Relu)
+            h_grouped[g] = hg
+
+        def quantise_h(g):
+            nc.vector.quantize_mx(
+                out=h_codes[:, g, :].bitcast(FP8X4), scales=h_planes[:, g, :], in_=h_grouped[g][:]
+            )
+
+        transposes(0)
+        edge_column(0)
+        scalar_copies(0)
+        vector_copies(0)
+
+        x_words = x_raw[:].bitcast(F32)
+        x_out = x_grouped[:].bitcast(F32).rearrange("w (c e u) -> w c e u", c=4, e=E, u=2)
+        x_bank0 = transpose_words(x_words, 0)
+        x_bank1 = transpose_words(x_words, 2)
+        copy_out(False, x_out[:, 0:2], x_bank0)
+        copy_out(True, x_out[:, 2:4], x_bank1)
+
+        edge_bank = psum.tile([P, 512], F32, name="edge_bank", tag="tp")
+        nc.tensor.matmul(edge_bank[:, 0:E], lhsT=ones[:], rhs=row[:, OUT : OUT + E], start=True, stop=True)
+        b1_bank = psum.tile([P, 512], F32, name="b1_bank", tag="tp")
+        for j in range(4):
+            nc.tensor.transpose(b1_bank[:, j * P : (j + 1) * P], b1_f32[:, j, :], ident[:])
+        nc.vector.tensor_copy(out=edge_all[:], in_=edge_bank[:, 0:E])
+        nc.vector.tensor_copy(
+            out=b1_col[:].rearrange("p g j -> p j g"),
+            in_=b1_bank[:].rearrange("p (j r) -> p j r", j=4)[:, :, 0:G],
+        )
+        nc.vector.quantize_mx(out=x_codes[:].bitcast(FP8X4), scales=x_planes[:], in_=x_grouped[:])
+
+        next_load = SLOTS
+        for s in range(1, UNITS + 4):
+            if s < UNITS:
+                transposes(s)
+                edge_column(s)
+            if s - 1 < UNITS:
+                quantise(s - 1)
+            if s >= 4 and s % 2 == 0:
+                add_terms((s - 4) // 2)
+            if s >= 5 and s % 2 == 1:
+                quantise_h((s - 5) // 2)
+            if s >= 3 and s % 2 == 1 and (s - 3) // 2 < G:
+                make_addend((s - 3) // 2)
+            if s < UNITS:
+                scalar_copies(s)
+                vector_copies(s)
+            if s >= 4 and s % 2 == 0:
+                relu((s - 4) // 2)
+            if s == UNITS:
+                for nq in range(4):
+                    cols = slice(nq * 512, (nq + 1) * 512)
+                    b2_bank = psum.tile([P, 512], F32, name="b2_bank", tag="tp")
+                    nc.tensor.matmul(b2_bank[:], lhsT=ones[:], rhs=row[:, cols], start=True, stop=True)
+                    nc.scalar.copy(out=b2_all[:, cols], in_=b2_bank[:])
+            if 0 <= s - 2 < UNITS:
+                layer1(s - 2)
+            if next_load < UNITS:
+                load_unit(next_load)
+            elif next_load < UNITS + G:
+                if next_load == UNITS:
+                    for a in range(2):
+                        for q in range(4):
+                            nc.sync.dma_start(
+                                out=w2_planes[32 * q : 32 * q + 16, a, :].bitcast(I32),
+                                in_=W2_scales[4 * a : 4 * a + 4, 4 * q : 4 * q + 4, :].bitcast(I32),
+                            )
+                load_w2(next_load - UNITS)
+            next_load += 1
+
+        acc = [psum.tile([P, 512], F32, name="acc%d" % nq, tag="tp") for nq in range(4)]
+        for g in range(G):
+            a, b = g // 4, g % 4
+            for nq in range(4):
+                cols = slice(nq * 512, (nq + 1) * 512)
+                nc.tensor.matmul_mx(
+                    out=acc[nq][:],
+                    lhsT=h_codes[:, g, :].bitcast(FP8X4),
+                    lhsT_scale=h_planes[:, g, :],
+                    rhs=w2_tiles[g][:, cols].bitcast(FP8X4),
+                    rhs_scale=w2_planes[4 * b : P, a, cols],
+                    start=(g == 0),
+                    stop=(g == G - 1),
+                )
+        for nq in range(4):
+            cols = slice(nq * 512, (nq + 1) * 512)
+            biased = fin.tile([P, 512], F32, name="biased", tag="biased")
+            nc.vector.tensor_tensor(out=biased[:], in0=acc[nq][:], in1=b2_all[:, cols], op=ADD)
+            result = fin.tile([P, 512], F32, name="result", tag="result")
+            nc.scalar.activation(out=result[:], in_=biased[:], func=ACT.Tanh)
+            nc.sync.dma_start(out=out[:, cols], in_=result[:])

@@ -87,14 +87,22 @@ def tile_edgenetwork_w_kernel(
         nc.vector.memset(warm_in[:], 0.0)
         nc.scalar.activation(out=warm_out[:], in_=warm_in[:], func=ACT.Tanh)
 
+        w2_planes = const.tile([P, 2, OUT], U8, name="w2_planes", align_bytes=64)
+        nc.vector.memset(w2_planes[:].bitcast(I32), 0)
+        scale_rows = W2_scales.rearrange("(a b) q n -> q b a n", a=2, b=4)
+        for q in range(16):
+            first = 32 * (q // 4) + q % 4
+            nc.gpsimd.dma_start(
+                out=w2_planes[first : first + 16 : 4, :, :].bitcast(F32),
+                in_=scale_rows[q].bitcast(F32),
+            )
+
         b1_rows = const.tile([P, 512], BF16, name="b1_rows")
         nc.vector.memset(b1_rows[:].bitcast(I32), 0)
         row = const.tile([P, OUT + E], BF16, name="row")
         nc.vector.memset(row[:].bitcast(I32), 0)
         ones = const.tile([P, P], BF16, name="ones")
         nc.vector.memset(ones[:], 1.0)
-        w2_planes = const.tile([P, 2, OUT], U8, name="w2_planes", align_bytes=64)
-        nc.vector.memset(w2_planes[:].bitcast(I32), 0)
 
         load_unit(0)
         nc.scalar.dma_start(out=b1_rows[0:G, :], in_=b1.rearrange("(g c) -> g c", g=G))
@@ -274,13 +282,6 @@ def tile_edgenetwork_w_kernel(
             if next_load < UNITS:
                 load_unit(next_load)
             elif next_load < UNITS + G:
-                if next_load == UNITS:
-                    for a in range(2):
-                        for q in range(4):
-                            nc.sync.dma_start(
-                                out=w2_planes[32 * q : 32 * q + 16, a, :].bitcast(I32),
-                                in_=W2_scales[4 * a : 4 * a + 4, 4 * q : 4 * q + 4, :].bitcast(I32),
-                            )
                 load_w2(next_load - UNITS)
             next_load += 1
 

@@ -48,7 +48,7 @@ def tile_edgenetwork_w_kernel(
         work = ctx.enter_context(tc.tile_pool(name="work", bufs=3))
         small = ctx.enter_context(tc.tile_pool(name="small", bufs=2))
         fin = ctx.enter_context(tc.tile_pool(name="fin", bufs=4))
-        psum = ctx.enter_context(tc.psum_pool(name="psum", bufs=6))
+        psum = ctx.enter_context(tc.psum_pool(name="psum", bufs=7))
 
         w1_view = W1.rearrange("(g p j) k -> g p j k", g=G, p=P, j=4)
 
@@ -87,22 +87,14 @@ def tile_edgenetwork_w_kernel(
         nc.vector.memset(warm_in[:], 0.0)
         nc.scalar.activation(out=warm_out[:], in_=warm_in[:], func=ACT.Tanh)
 
-        w2_planes = const.tile([P, 2, OUT], U8, name="w2_planes", align_bytes=64)
-        nc.vector.memset(w2_planes[:].bitcast(I32), 0)
-        scale_rows = W2_scales.rearrange("(a b) q n -> q b a n", a=2, b=4)
-        for q in range(16):
-            first = 32 * (q // 4) + q % 4
-            nc.gpsimd.dma_start(
-                out=w2_planes[first : first + 16 : 4, :, :].bitcast(F32),
-                in_=scale_rows[q].bitcast(F32),
-            )
-
         b1_rows = const.tile([P, 512], BF16, name="b1_rows")
         nc.vector.memset(b1_rows[:].bitcast(I32), 0)
         row = const.tile([P, OUT + E], BF16, name="row")
         nc.vector.memset(row[:].bitcast(I32), 0)
         ones = const.tile([P, P], BF16, name="ones")
         nc.vector.memset(ones[:], 1.0)
+        w2_planes = const.tile([P, 2, OUT], U8, name="w2_planes", align_bytes=64)
+        nc.vector.memset(w2_planes[:].bitcast(I32), 0)
 
         load_unit(0)
         nc.scalar.dma_start(out=b1_rows[0:G, :], in_=b1.rearrange("(g c) -> g c", g=G))
@@ -114,8 +106,30 @@ def tile_edgenetwork_w_kernel(
         nc.sync.dma_start(out=x_raw[:, 256:1024], in_=dst_node_hidden)
         nc.sync.dma_start(out=x_raw[:, 1024:1280], in_=src_node_feat)
         nc.sync.dma_start(out=x_raw[:, 1280:2048], in_=src_node_hidden)
-        for s in range(1, SLOTS):
-            load_unit(s)
+        loads = []
+        for s in range(1, UNITS):
+            loads.append(("w1", s))
+            if s >= 7 and s % 2 == 1:
+                loads.append(("w2", (s - 7) // 2))
+        for g in range(5, G):
+            loads.append(("w2", g))
+
+        def issue(load):
+            kind, index = load
+            if kind == "w1":
+                load_unit(index)
+            else:
+                if index == 0:
+                    for a in range(2):
+                        for q in range(4):
+                            nc.sync.dma_start(
+                                out=w2_planes[32 * q : 32 * q + 16, a, :].bitcast(I32),
+                                in_=W2_scales[4 * a : 4 * a + 4, 4 * q : 4 * q + 4, :].bitcast(I32),
+                            )
+                load_w2(index)
+
+        for i in range(SLOTS - 1):
+            issue(loads[i])
 
         b1_f32 = const.tile([P, 4, P], F32, name="b1_f32")
         nc.vector.tensor_copy(out=b1_f32[:], in_=b1_rows[:].rearrange("r (p j) -> r j p", j=4))
@@ -123,7 +137,7 @@ def tile_edgenetwork_w_kernel(
         w1_edge = const.tile([P, G, 4], F32, name="w1_edge")
         b1_col = const.tile([P, G, 4], F32, name="b1_col")
         edge_all = const.tile([P, E], F32, name="edge_all")
-        b2_all = const.tile([P, OUT], F32, name="b2_all")
+        b2_all = const.tile([P, OUT], BF16, name="b2_all")
         x_grouped = const.tile([P, D], BF16, name="x_grouped", align_bytes=64)
         x_codes = const.tile([P, D // 4], U32, name="x_codes", align_bytes=64)
         x_planes = const.tile([P, D // 4], U8, name="x_planes", align_bytes=64)
@@ -158,18 +172,14 @@ def tile_edgenetwork_w_kernel(
             g, jh = s // 2, s % 2
             nc.vector.tensor_copy(out=w1_edge[:, g, 2 * jh : 2 * jh + 2], in_=raw[s][:, :, D])
 
-        def scalar_copies(s):
+        def copies(s):
             gr = work.tile([P, 4096], BF16, name="grouped", tag="grouped", align_bytes=64)
             grouped[s] = gr
             words = gr[:].bitcast(F32).rearrange("w (o p u) -> w o p u", o=8, p=P, u=2)
-            last = 3 if s % 2 == 0 else 4
-            for b in range(last):
-                copy_out(False, words[:, 2 * b : 2 * b + 2], banks[s][b])
-
-        def vector_copies(s):
             if s % 2 == 0:
-                words = grouped[s][:].bitcast(F32).rearrange("w (o p u) -> w o p u", o=8, p=P, u=2)
-                copy_out(True, words[:, 6:8], banks[s][3])
+                copy_out(True, words[:, 0:2], banks[s][0])
+            for b in range(1 if s % 2 == 0 else 0, 4):
+                copy_out(False, words[:, 2 * b : 2 * b + 2], banks[s][b])
 
         def quantise(s):
             c = work.tile([P, 1024], U32, name="codes", tag="codes", align_bytes=64)
@@ -181,7 +191,7 @@ def tile_edgenetwork_w_kernel(
         def layer1(s):
             g, jh = s // 2, s % 2
             if jh == 0:
-                hidden[g] = psum.tile([P, 512], F32, name="hp", tag="hp", bufs=2)
+                hidden[g] = psum.tile([P, 512], F32, name="hp", tag="hp", bufs=1)
             for jj in range(2):
                 j = 2 * jh + jj
                 for c in range(4):
@@ -230,9 +240,8 @@ def tile_edgenetwork_w_kernel(
             )
 
         transposes(0)
+        copies(0)
         edge_column(0)
-        scalar_copies(0)
-        vector_copies(0)
 
         x_words = x_raw[:].bitcast(F32)
         x_out = x_grouped[:].bitcast(F32).rearrange("w (c e u) -> w c e u", c=4, e=E, u=2)
@@ -253,40 +262,12 @@ def tile_edgenetwork_w_kernel(
         )
         nc.vector.quantize_mx(out=x_codes[:].bitcast(FP8X4), scales=x_planes[:], in_=x_grouped[:])
 
-        next_load = SLOTS
-        for s in range(1, UNITS + 4):
-            if s < UNITS:
-                transposes(s)
-                edge_column(s)
-            if s - 1 < UNITS:
-                quantise(s - 1)
-            if s >= 4 and s % 2 == 0:
-                add_terms((s - 4) // 2)
-            if s >= 5 and s % 2 == 1:
-                quantise_h((s - 5) // 2)
-            if s >= 3 and s % 2 == 1 and (s - 3) // 2 < G:
-                make_addend((s - 3) // 2)
-            if s < UNITS:
-                scalar_copies(s)
-                vector_copies(s)
-            if s >= 4 and s % 2 == 0:
-                relu((s - 4) // 2)
-            if s == UNITS:
-                for nq in range(4):
-                    cols = slice(nq * 512, (nq + 1) * 512)
-                    b2_bank = psum.tile([P, 512], F32, name="b2_bank", tag="tp")
-                    nc.tensor.matmul(b2_bank[:], lhsT=ones[:], rhs=row[:, cols], start=True, stop=True)
-                    nc.scalar.copy(out=b2_all[:, cols], in_=b2_bank[:])
-            if 0 <= s - 2 < UNITS:
-                layer1(s - 2)
-            if next_load < UNITS:
-                load_unit(next_load)
-            elif next_load < UNITS + G:
-                load_w2(next_load - UNITS)
-            next_load += 1
+        acc = []
 
-        acc = [psum.tile([P, 512], F32, name="acc%d" % nq, tag="tp") for nq in range(4)]
-        for g in range(G):
+        def layer2(g):
+            if g == 0:
+                for nq in range(4):
+                    acc.append(psum.tile([P, 512], F32, name="acc%d" % nq, tag="tp"))
             a, b = g // 4, g % 4
             for nq in range(4):
                 cols = slice(nq * 512, (nq + 1) * 512)
@@ -299,6 +280,48 @@ def tile_edgenetwork_w_kernel(
                     start=(g == 0),
                     stop=(g == G - 1),
                 )
+
+        position = SLOTS - 1
+        for s in range(1, UNITS + 4):
+            if s < UNITS:
+                transposes(s)
+                copies(s)
+            if s >= 4 and s % 2 == 0:
+                add_terms((s - 4) // 2)
+                relu((s - 4) // 2)
+            if s < UNITS:
+                edge_column(s)
+            if s - 1 < UNITS:
+                quantise(s - 1)
+            if s >= 5 and s % 2 == 1:
+                quantise_h((s - 5) // 2)
+            if s >= 3 and s % 2 == 1 and (s - 3) // 2 < G:
+                make_addend((s - 3) // 2)
+            if 0 <= s - 2 < UNITS:
+                layer1(s - 2)
+            if s >= 8 and s % 2 == 0 and s <= UNITS:
+                layer2((s - 8) // 2)
+            if s == UNITS:
+                for half in range(2):
+                    b2_bank = psum.tile([P, 1024], BF16, name="b2_bank", tag="tp")
+                    for i in range(2):
+                        first = 1024 * half + 512 * i
+                        nc.tensor.matmul(
+                            b2_bank[:, 512 * i : 512 * (i + 1)],
+                            lhsT=ones[:],
+                            rhs=row[:, first : first + 512],
+                            start=True,
+                            stop=True,
+                        )
+                    nc.scalar.copy(out=b2_all[:, 1024 * half : 1024 * (half + 1)], in_=b2_bank[:])
+            if s == UNITS + 1:
+                layer2(5)
+            if position < len(loads):
+                issue(loads[position])
+                position += 1
+
+        layer2(6)
+        layer2(7)
         for nq in range(4):
             cols = slice(nq * 512, (nq + 1) * 512)
             biased = fin.tile([P, 512], F32, name="biased", tag="biased")

@@ -11,6 +11,7 @@ U8 = mybir.dt.uint8
 FP8X4 = mybir.dt.float8_e4m3fn_x4
 ADD = mybir.AluOpType.add
 MULT = mybir.AluOpType.mult
+MAX = mybir.AluOpType.max
 ACT = mybir.ActivationFunctionType
 
 P = 128
@@ -48,7 +49,7 @@ def tile_edgenetwork_w_kernel(
         work = ctx.enter_context(tc.tile_pool(name="work", bufs=3))
         small = ctx.enter_context(tc.tile_pool(name="small", bufs=2))
         fin = ctx.enter_context(tc.tile_pool(name="fin", bufs=4))
-        psum = ctx.enter_context(tc.psum_pool(name="psum", bufs=7))
+        psum = ctx.enter_context(tc.psum_pool(name="psum", bufs=6))
 
         w1_view = W1.rearrange("(g p j) k -> g p j k", g=G, p=P, j=4)
 
@@ -106,13 +107,7 @@ def tile_edgenetwork_w_kernel(
         nc.sync.dma_start(out=x_raw[:, 256:1024], in_=dst_node_hidden)
         nc.sync.dma_start(out=x_raw[:, 1024:1280], in_=src_node_feat)
         nc.sync.dma_start(out=x_raw[:, 1280:2048], in_=src_node_hidden)
-        loads = []
-        for s in range(1, UNITS):
-            loads.append(("w1", s))
-            if s >= 7 and s % 2 == 1:
-                loads.append(("w2", (s - 7) // 2))
-        for g in range(5, G):
-            loads.append(("w2", g))
+        loads = [("w1", s) for s in range(1, UNITS)] + [("w2", g) for g in range(G)]
 
         def issue(load):
             kind, index = load
@@ -176,9 +171,7 @@ def tile_edgenetwork_w_kernel(
             gr = work.tile([P, 4096], BF16, name="grouped", tag="grouped", align_bytes=64)
             grouped[s] = gr
             words = gr[:].bitcast(F32).rearrange("w (o p u) -> w o p u", o=8, p=P, u=2)
-            if s % 2 == 0:
-                copy_out(True, words[:, 0:2], banks[s][0])
-            for b in range(1 if s % 2 == 0 else 0, 4):
+            for b in range(4):
                 copy_out(False, words[:, 2 * b : 2 * b + 2], banks[s][b])
 
         def quantise(s):
@@ -191,7 +184,7 @@ def tile_edgenetwork_w_kernel(
         def layer1(s):
             g, jh = s // 2, s % 2
             if jh == 0:
-                hidden[g] = psum.tile([P, 512], F32, name="hp", tag="hp", bufs=1)
+                hidden[g] = psum.tile([P, 512], F32, name="hp", tag="hp", bufs=2)
             for jj in range(2):
                 j = 2 * jh + jj
                 for c in range(4):
@@ -231,7 +224,9 @@ def tile_edgenetwork_w_kernel(
 
         def relu(g):
             hg = small.tile([P, 4 * E], BF16, name="h_grouped", tag="h_grouped", align_bytes=64)
-            nc.scalar.activation(out=hg[:], in_=pre[g][:].rearrange("p e j -> p (e j)"), func=ACT.Relu)
+            nc.vector.tensor_scalar(
+                out=hg[:], in0=pre[g][:].rearrange("p e j -> p (e j)"), scalar1=0.0, scalar2=None, op0=MAX
+            )
             h_grouped[g] = hg
 
         def quantise_h(g):
@@ -299,9 +294,12 @@ def tile_edgenetwork_w_kernel(
                 make_addend((s - 3) // 2)
             if 0 <= s - 2 < UNITS:
                 layer1(s - 2)
-            if s >= 8 and s % 2 == 0 and s <= UNITS:
-                layer2((s - 8) // 2)
             if s == UNITS:
+                layer2(0)
+            if s == UNITS + 1:
+                layer2(1)
+                layer2(2)
+            if s == UNITS + 2:
                 for half in range(2):
                     b2_bank = psum.tile([P, 1024], BF16, name="b2_bank", tag="tp")
                     for i in range(2):
@@ -314,14 +312,12 @@ def tile_edgenetwork_w_kernel(
                             stop=True,
                         )
                     nc.scalar.copy(out=b2_all[:, 1024 * half : 1024 * (half + 1)], in_=b2_bank[:])
-            if s == UNITS + 1:
-                layer2(5)
             if position < len(loads):
                 issue(loads[position])
                 position += 1
 
-        layer2(6)
-        layer2(7)
+        for g in range(3, G):
+            layer2(g)
         for nq in range(4):
             cols = slice(nq * 512, (nq + 1) * 512)
             biased = fin.tile([P, 512], F32, name="biased", tag="biased")

@@ -23,6 +23,7 @@ G = MID // 512
 UNITS = 2 * G
 ROW_PITCH = 2064
 SLOTS = 14
+PIECES = ((0, 512), (512, 512), (1024, 512), (1536, 256), (1792, 128), (1920, 128))
 
 FLOPS = 2 * E * (D + 1) * MID + 2 * E * MID * OUT
 
@@ -76,8 +77,8 @@ def tile_edgenetwork_w_kernel(
             if g < G - 1:
                 nc.sync.dma_start(out=w[:].bitcast(I32), in_=src)
             else:
-                for nq in range(4):
-                    cols = slice(nq * 512, (nq + 1) * 512)
+                for first, width in PIECES:
+                    cols = slice(first, first + width)
                     nc.sync.dma_start(out=w[:, cols].bitcast(I32), in_=src[:, cols])
             w2_tiles[g] = w
 
@@ -261,13 +262,13 @@ def tile_edgenetwork_w_kernel(
 
         def layer2(g):
             if g == 0:
-                for nq in range(4):
-                    acc.append(psum.tile([P, 512], F32, name="acc%d" % nq, tag="tp"))
+                for i in range(len(PIECES)):
+                    acc.append(psum.tile([P, 512], F32, name="acc%d" % i, tag="tp"))
             a, b = g // 4, g % 4
-            for nq in range(4):
-                cols = slice(nq * 512, (nq + 1) * 512)
+            for i, (first, width) in enumerate(PIECES):
+                cols = slice(first, first + width)
                 nc.tensor.matmul_mx(
-                    out=acc[nq][:],
+                    out=acc[i][:, 0:width],
                     lhsT=h_codes[:, g, :].bitcast(FP8X4),
                     lhsT_scale=h_planes[:, g, :],
                     rhs=w2_tiles[g][:, cols].bitcast(FP8X4),
@@ -301,7 +302,7 @@ def tile_edgenetwork_w_kernel(
                 layer2(2)
             if s == UNITS + 2:
                 for half in range(2):
-                    b2_bank = psum.tile([P, 1024], BF16, name="b2_bank", tag="tp")
+                    b2_bank = psum.tile([P, 1024], BF16, name="b2_bank", tag="hp", bufs=2)
                     for i in range(2):
                         first = 1024 * half + 512 * i
                         nc.tensor.matmul(
@@ -318,10 +319,10 @@ def tile_edgenetwork_w_kernel(
 
         for g in range(3, G):
             layer2(g)
-        for nq in range(4):
-            cols = slice(nq * 512, (nq + 1) * 512)
+        for i, (first, width) in enumerate(PIECES):
+            cols = slice(first, first + width)
             biased = fin.tile([P, 512], F32, name="biased", tag="biased")
-            nc.vector.tensor_tensor(out=biased[:], in0=acc[nq][:], in1=b2_all[:, cols], op=ADD)
+            nc.vector.tensor_tensor(out=biased[:, 0:width], in0=acc[i][:, 0:width], in1=b2_all[:, cols], op=ADD)
             result = fin.tile([P, 512], F32, name="result", tag="result")
-            nc.scalar.activation(out=result[:], in_=biased[:], func=ACT.Tanh)
-            nc.sync.dma_start(out=out[:, cols], in_=result[:])
+            nc.scalar.activation(out=result[:, 0:width], in_=biased[:, 0:width], func=ACT.Tanh)
+            nc.sync.dma_start(out=out[:, cols], in_=result[:, 0:width])

@@ -23,7 +23,7 @@ G = MID // 512
 UNITS = 2 * G
 ROW_PITCH = 2064
 SLOTS = 14
-PIECES = ((0, 512), (512, 512), (1024, 512), (1536, 256), (1792, 128), (1920, 128))
+SPLIT_UNITS = 3
 
 FLOPS = 2 * E * (D + 1) * MID + 2 * E * MID * OUT
 
@@ -68,7 +68,12 @@ def tile_edgenetwork_w_kernel(
         def load_unit(s):
             r = big.tile([P, 2, ROW_PITCH], BF16, name="raw", tag="big", align_bytes=64)
             g, jh = s // 2, s % 2
-            nc.sync.dma_start(out=r[:, :, 0 : D + 1], in_=w1_view[g][:, 2 * jh : 2 * jh + 2, :])
+            if s < SPLIT_UNITS:
+                for jj in range(2):
+                    nc.sync.dma_start(out=r[:, jj, 0:1024], in_=w1_view[g][:, 2 * jh + jj, 0:1024])
+                    nc.sync.dma_start(out=r[:, jj, 1024 : D + 1], in_=w1_view[g][:, 2 * jh + jj, 1024 : D + 1])
+            else:
+                nc.sync.dma_start(out=r[:, :, 0 : D + 1], in_=w1_view[g][:, 2 * jh : 2 * jh + 2, :])
             raw[s] = r
 
         def load_w2(g):
@@ -77,8 +82,8 @@ def tile_edgenetwork_w_kernel(
             if g < G - 1:
                 nc.sync.dma_start(out=w[:].bitcast(I32), in_=src)
             else:
-                for first, width in PIECES:
-                    cols = slice(first, first + width)
+                for nq in range(4):
+                    cols = slice(nq * 512, (nq + 1) * 512)
                     nc.sync.dma_start(out=w[:, cols].bitcast(I32), in_=src[:, cols])
             w2_tiles[g] = w
 
@@ -257,18 +262,30 @@ def tile_edgenetwork_w_kernel(
             in_=b1_bank[:].rearrange("p (j r) -> p j r", j=4)[:, :, 0:G],
         )
         nc.vector.quantize_mx(out=x_codes[:].bitcast(FP8X4), scales=x_planes[:], in_=x_grouped[:])
+        for half in range(2):
+            b2_bank = psum.tile([P, 1024], BF16, name="b2_bank", tag="tp")
+            for i in range(2):
+                first = 1024 * half + 512 * i
+                nc.tensor.matmul(
+                    b2_bank[:, 512 * i : 512 * (i + 1)],
+                    lhsT=ones[:],
+                    rhs=row[:, first : first + 512],
+                    start=True,
+                    stop=True,
+                )
+            nc.scalar.copy(out=b2_all[:, 1024 * half : 1024 * (half + 1)], in_=b2_bank[:])
 
         acc = []
 
         def layer2(g):
             if g == 0:
-                for i in range(len(PIECES)):
-                    acc.append(psum.tile([P, 512], F32, name="acc%d" % i, tag="tp"))
+                for nq in range(4):
+                    acc.append(psum.tile([P, 512], F32, name="acc%d" % nq, tag="tp"))
             a, b = g // 4, g % 4
-            for i, (first, width) in enumerate(PIECES):
-                cols = slice(first, first + width)
+            for nq in range(4):
+                cols = slice(nq * 512, (nq + 1) * 512)
                 nc.tensor.matmul_mx(
-                    out=acc[i][:, 0:width],
+                    out=acc[nq][:],
                     lhsT=h_codes[:, g, :].bitcast(FP8X4),
                     lhsT_scale=h_planes[:, g, :],
                     rhs=w2_tiles[g][:, cols].bitcast(FP8X4),
@@ -300,29 +317,16 @@ def tile_edgenetwork_w_kernel(
             if s == UNITS + 1:
                 layer2(1)
                 layer2(2)
-            if s == UNITS + 2:
-                for half in range(2):
-                    b2_bank = psum.tile([P, 1024], BF16, name="b2_bank", tag="hp", bufs=2)
-                    for i in range(2):
-                        first = 1024 * half + 512 * i
-                        nc.tensor.matmul(
-                            b2_bank[:, 512 * i : 512 * (i + 1)],
-                            lhsT=ones[:],
-                            rhs=row[:, first : first + 512],
-                            start=True,
-                            stop=True,
-                        )
-                    nc.scalar.copy(out=b2_all[:, 1024 * half : 1024 * (half + 1)], in_=b2_bank[:])
             if position < len(loads):
                 issue(loads[position])
                 position += 1
 
         for g in range(3, G):
             layer2(g)
-        for i, (first, width) in enumerate(PIECES):
-            cols = slice(first, first + width)
+        for nq in range(4):
+            cols = slice(nq * 512, (nq + 1) * 512)
             biased = fin.tile([P, 512], F32, name="biased", tag="biased")
-            nc.vector.tensor_tensor(out=biased[:, 0:width], in0=acc[i][:, 0:width], in1=b2_all[:, cols], op=ADD)
+            nc.vector.tensor_tensor(out=biased[:], in0=acc[nq][:], in1=b2_all[:, cols], op=ADD)
             result = fin.tile([P, 512], F32, name="result", tag="result")
-            nc.scalar.activation(out=result[:, 0:width], in_=biased[:, 0:width], func=ACT.Tanh)
-            nc.sync.dma_start(out=out[:, cols], in_=result[:, 0:width])
+            nc.scalar.activation(out=result[:], in_=biased[:], func=ACT.Tanh)
+            nc.sync.dma_start(out=out[:, cols], in_=result[:])

@@ -23,7 +23,6 @@ G = MID // 512
 UNITS = 2 * G
 ROW_PITCH = 2064
 SLOTS = 14
-SPLIT_UNITS = 3
 
 FLOPS = 2 * E * (D + 1) * MID + 2 * E * MID * OUT
 
@@ -68,23 +67,13 @@ def tile_edgenetwork_w_kernel(
         def load_unit(s):
             r = big.tile([P, 2, ROW_PITCH], BF16, name="raw", tag="big", align_bytes=64)
             g, jh = s // 2, s % 2
-            if s < SPLIT_UNITS:
-                for jj in range(2):
-                    nc.sync.dma_start(out=r[:, jj, 0:1024], in_=w1_view[g][:, 2 * jh + jj, 0:1024])
-                    nc.sync.dma_start(out=r[:, jj, 1024 : D + 1], in_=w1_view[g][:, 2 * jh + jj, 1024 : D + 1])
-            else:
-                nc.sync.dma_start(out=r[:, :, 0 : D + 1], in_=w1_view[g][:, 2 * jh : 2 * jh + 2, :])
+            nc.sync.dma_start(out=r[:, :, 0 : D + 1], in_=w1_view[g][:, 2 * jh : 2 * jh + 2, :])
             raw[s] = r
 
         def load_w2(g):
             w = big.tile([P, OUT], U32, name="w2", tag="big", align_bytes=64)
             src = W2_words[g].rearrange("p n t -> p (n t)").bitcast(I32)
-            if g < G - 1:
-                nc.sync.dma_start(out=w[:].bitcast(I32), in_=src)
-            else:
-                for nq in range(4):
-                    cols = slice(nq * 512, (nq + 1) * 512)
-                    nc.sync.dma_start(out=w[:, cols].bitcast(I32), in_=src[:, cols])
+            nc.sync.dma_start(out=w[:].bitcast(I32), in_=src)
             w2_tiles[g] = w
 
         ident = const.tile([P, P], F32, name="ident")
@@ -262,18 +251,6 @@ def tile_edgenetwork_w_kernel(
             in_=b1_bank[:].rearrange("p (j r) -> p j r", j=4)[:, :, 0:G],
         )
         nc.vector.quantize_mx(out=x_codes[:].bitcast(FP8X4), scales=x_planes[:], in_=x_grouped[:])
-        for half in range(2):
-            b2_bank = psum.tile([P, 1024], BF16, name="b2_bank", tag="tp")
-            for i in range(2):
-                first = 1024 * half + 512 * i
-                nc.tensor.matmul(
-                    b2_bank[:, 512 * i : 512 * (i + 1)],
-                    lhsT=ones[:],
-                    rhs=row[:, first : first + 512],
-                    start=True,
-                    stop=True,
-                )
-            nc.scalar.copy(out=b2_all[:, 1024 * half : 1024 * (half + 1)], in_=b2_bank[:])
 
         acc = []
 
@@ -317,6 +294,19 @@ def tile_edgenetwork_w_kernel(
             if s == UNITS + 1:
                 layer2(1)
                 layer2(2)
+            if s == UNITS + 2:
+                for half in range(2):
+                    b2_bank = psum.tile([P, 1024], BF16, name="b2_bank", tag="tp")
+                    for i in range(2):
+                        first = 1024 * half + 512 * i
+                        nc.tensor.matmul(
+                            b2_bank[:, 512 * i : 512 * (i + 1)],
+                            lhsT=ones[:],
+                            rhs=row[:, first : first + 512],
+                            start=True,
+                            stop=True,
+                        )
+                    nc.scalar.copy(out=b2_all[:, 1024 * half : 1024 * (half + 1)], in_=b2_bank[:])
             if position < len(loads):
                 issue(loads[position])
                 position += 1

from contextlib import ExitStack

import concourse.mybir as mybir
from concourse.masks import make_identity

F32 = mybir.dt.float32
BF16 = mybir.dt.bfloat16
I32 = mybir.dt.int32
U32 = mybir.dt.uint32
U8 = mybir.dt.uint8
FP8X4 = mybir.dt.float8_e4m3fn_x4
ADD = mybir.AluOpType.add
MULT = mybir.AluOpType.mult
MAX = mybir.AluOpType.max
ACT = mybir.ActivationFunctionType

P = 128
E = 128
D = 2048
MID = 4096
OUT = 2048
G = MID // 512
UNITS = 2 * G
ROW_PITCH = 2064
SLOTS = 14

FLOPS = 2 * E * (D + 1) * MID + 2 * E * MID * OUT


def tile_edgenetwork_w_kernel(
    tc,
    dst_node_feat,
    dst_node_hidden,
    src_node_feat,
    src_node_hidden,
    edge_feat,
    W1,
    b1,
    W2_words,
    W2_scales,
    b2,
    out,
):
    nc = tc.nc
    with ExitStack() as ctx:
        ctx.enter_context(tc.manual_schedule())
        const = ctx.enter_context(tc.tile_pool(name="const", bufs=1))
        big = ctx.enter_context(tc.tile_pool(name="big", bufs=SLOTS))
        work = ctx.enter_context(tc.tile_pool(name="work", bufs=3))
        small = ctx.enter_context(tc.tile_pool(name="small", bufs=2))
        fin = ctx.enter_context(tc.tile_pool(name="fin", bufs=4))
        psum = ctx.enter_context(tc.psum_pool(name="psum", bufs=6))

        w1_view = W1.rearrange("(g p j) k -> g p j k", g=G, p=P, j=4)

        raw = {}
        banks = {}
        grouped = {}
        codes = {}
        planes1 = {}
        hidden = {}
        addend = {}
        pre = {}
        h_grouped = {}
        w2_tiles = {}

        def load_unit(s):
            r = big.tile([P, 2, ROW_PITCH], BF16, name="raw", tag="big", align_bytes=64)
            g, jh = s // 2, s % 2
            nc.sync.dma_start(out=r[:, :, 0 : D + 1], in_=w1_view[g][:, 2 * jh : 2 * jh + 2, :])
            raw[s] = r

        def load_w2(g):
            w = big.tile([P, OUT], U32, name="w2", tag="big", align_bytes=64)
            src = W2_words[g].rearrange("p n t -> p (n t)").bitcast(I32)
            nc.sync.dma_start(out=w[:].bitcast(I32), in_=src)
            w2_tiles[g] = w

        ident = const.tile([P, P], F32, name="ident")
        make_identity(nc, ident[:])
        warm_in = const.tile([P, 1], F32, name="warm_in")
        warm_out = const.tile([P, 1], F32, name="warm_out")
        nc.vector.memset(warm_in[:], 0.0)
        nc.scalar.activation(out=warm_out[:], in_=warm_in[:], func=ACT.Tanh)

        b1_rows = const.tile([P, 512], BF16, name="b1_rows")
        nc.vector.memset(b1_rows[:].bitcast(I32), 0)
        row = const.tile([P, OUT + E], BF16, name="row")
        nc.vector.memset(row[:].bitcast(I32), 0)
        ones = const.tile([P, P], BF16, name="ones")
        nc.vector.memset(ones[:], 1.0)
        w2_planes = const.tile([P, 2, OUT], U8, name="w2_planes", align_bytes=64)
        nc.vector.memset(w2_planes[:].bitcast(I32), 0)

        load_unit(0)
        nc.scalar.dma_start(out=b1_rows[0:G, :], in_=b1.rearrange("(g c) -> g c", g=G))
        nc.scalar.dma_start(out=row[0:1, OUT : OUT + E], in_=edge_feat.rearrange("(o n) -> o n", o=1))
        nc.scalar.dma_start(out=row[0:1, 0:OUT], in_=b2.rearrange("(o n) -> o n", o=1))

        x_raw = const.tile([P, D], BF16, name="x_raw")
        nc.sync.dma_start(out=x_raw[:, 0:256], in_=dst_node_feat)
        nc.sync.dma_start(out=x_raw[:, 256:1024], in_=dst_node_hidden)
        nc.sync.dma_start(out=x_raw[:, 1024:1280], in_=src_node_feat)
        nc.sync.dma_start(out=x_raw[:, 1280:2048], in_=src_node_hidden)
        loads = [("w1", s) for s in range(1, UNITS)] + [("w2", g) for g in range(G)]

        def issue(load):
            kind, index = load
            if kind == "w1":
                load_unit(index)
            else:
                if index == 0:
                    for a in range(2):
                        for q in range(4):
                            nc.sync.dma_start(
                                out=w2_planes[32 * q : 32 * q + 16, a, :].bitcast(I32),
                                in_=W2_scales[4 * a : 4 * a + 4, 4 * q : 4 * q + 4, :].bitcast(I32),
                            )
                load_w2(index)

        for i in range(SLOTS - 1):
            issue(loads[i])

        b1_f32 = const.tile([P, 4, P], F32, name="b1_f32")
        nc.vector.tensor_copy(out=b1_f32[:], in_=b1_rows[:].rearrange("r (p j) -> r j p", j=4))

        w1_edge = const.tile([P, G, 4], F32, name="w1_edge")
        b1_col = const.tile([P, G, 4], F32, name="b1_col")
        edge_all = const.tile([P, E], F32, name="edge_all")
        b2_all = const.tile([P, OUT], BF16, name="b2_all")
        x_grouped = const.tile([P, D], BF16, name="x_grouped", align_bytes=64)
        x_codes = const.tile([P, D // 4], U32, name="x_codes", align_bytes=64)
        x_planes = const.tile([P, D // 4], U8, name="x_planes", align_bytes=64)
        h_codes = const.tile([P, G, E], U32, name="h_codes", align_bytes=64)
        h_planes = const.tile([P, G, E], U8, name="h_planes", align_bytes=64)

        def transpose_words(src_words, first_pass):
            bank = psum.tile([P, 512], F32, name="tp", tag="tp")
            for cc in range(2):
                for u in range(2):
                    col = 256 * (first_pass + cc) + 128 * u
                    nc.tensor.transpose(
                        bank[:, (2 * cc + u) * P : (2 * cc + u + 1) * P],
                        src_words[:, col : col + P],
                        ident[:],
                    )
            return bank

        def copy_out(engine_is_vector, dst_words, bank):
            src = bank[:].rearrange("w (c u p) -> w c p u", c=2, u=2, p=P)
            if engine_is_vector:
                nc.vector.tensor_copy(out=dst_words, in_=src)
            else:
                nc.scalar.copy(out=dst_words, in_=src)

        def transposes(s):
            banks[s] = [
                transpose_words(raw[s][:, b // 2, 0:D].bitcast(F32), 2 * (b % 2)) for b in range(4)
            ]

        def edge_column(s):
            g, jh = s // 2, s % 2
            nc.vector.tensor_copy(out=w1_edge[:, g, 2 * jh : 2 * jh + 2], in_=raw[s][:, :, D])

        def copies(s):
            gr = work.tile([P, 4096], BF16, name="grouped", tag="grouped", align_bytes=64)
            grouped[s] = gr
            words = gr[:].bitcast(F32).rearrange("w (o p u) -> w o p u", o=8, p=P, u=2)
            for b in range(4):
                copy_out(False, words[:, 2 * b : 2 * b + 2], banks[s][b])

        def quantise(s):
            c = work.tile([P, 1024], U32, name="codes", tag="codes", align_bytes=64)
            pl = work.tile([P, 1024], U8, name="planes", tag="planes", align_bytes=64)
            nc.vector.quantize_mx(out=c[:].bitcast(FP8X4), scales=pl[:], in_=grouped[s][:])
            codes[s] = c
            planes1[s] = pl

        def layer1(s):
            g, jh = s // 2, s % 2
            if jh == 0:
                hidden[g] = psum.tile([P, 512], F32, name="hp", tag="hp", bufs=2)
            for jj in range(2):
                j = 2 * jh + jj
                for c in range(4):
                    o = 4 * jj + c
                    nc.tensor.matmul_mx(
                        out=hidden[g][:, j * E : (j + 1) * E],
                        lhsT=codes[s][:, o * P : (o + 1) * P].bitcast(FP8X4),
                        lhsT_scale=planes1[s][:, o * P : (o + 1) * P],
                        rhs=x_codes[:, c * E : (c + 1) * E].bitcast(FP8X4),
                        rhs_scale=x_planes[:, c * E : (c + 1) * E],
                        start=(c == 0),
                        stop=(c == 3),
                    )

        def make_addend(g):
            a = small.tile([P, 4, E], F32, name="addend", tag="addend")
            for j in range(4):
                nc.vector.tensor_scalar(
                    out=a[:, j, :],
                    in0=edge_all[:],
                    scalar1=w1_edge[:, g, j : j + 1],
                    scalar2=b1_col[:, g, j : j + 1],
                    op0=MULT,
                    op1=ADD,
                )
            addend[g] = a

        def add_terms(g):
            z = small.tile([P, E, 4], F32, name="pre", tag="pre")
            nc.vector.tensor_tensor(
                out=z[:],
                in0=hidden[g][:].rearrange("p (j e) -> p e j", j=4),
                in1=addend[g][:].rearrange("p j e -> p e j"),
                op=ADD,
            )
            pre[g] = z

        def relu(g):
            hg = small.tile([P, 4 * E], BF16, name="h_grouped", tag="h_grouped", align_bytes=64)
            nc.vector.tensor_scalar(
                out=hg[:], in0=pre[g][:].rearrange("p e j -> p (e j)"), scalar1=0.0, scalar2=None, op0=MAX
            )
            h_grouped[g] = hg

        def quantise_h(g):
            nc.vector.quantize_mx(
                out=h_codes[:, g, :].bitcast(FP8X4), scales=h_planes[:, g, :], in_=h_grouped[g][:]
            )

        transposes(0)
        copies(0)
        edge_column(0)

        x_words = x_raw[:].bitcast(F32)
        x_out = x_grouped[:].bitcast(F32).rearrange("w (c e u) -> w c e u", c=4, e=E, u=2)
        x_bank0 = transpose_words(x_words, 0)
        x_bank1 = transpose_words(x_words, 2)
        copy_out(False, x_out[:, 0:2], x_bank0)
        copy_out(True, x_out[:, 2:4], x_bank1)

        edge_bank = psum.tile([P, 512], F32, name="edge_bank", tag="tp")
        nc.tensor.matmul(edge_bank[:, 0:E], lhsT=ones[:], rhs=row[:, OUT : OUT + E], start=True, stop=True)
        b1_bank = psum.tile([P, 512], F32, name="b1_bank", tag="tp")
        for j in range(4):
            nc.tensor.transpose(b1_bank[:, j * P : (j + 1) * P], b1_f32[:, j, :], ident[:])
        nc.vector.tensor_copy(out=edge_all[:], in_=edge_bank[:, 0:E])
        nc.vector.tensor_copy(
            out=b1_col[:].rearrange("p g j -> p j g"),
            in_=b1_bank[:].rearrange("p (j r) -> p j r", j=4)[:, :, 0:G],
        )
        nc.vector.quantize_mx(out=x_codes[:].bitcast(FP8X4), scales=x_planes[:], in_=x_grouped[:])

        acc = []

        def layer2(g):
            if g == 0:
                for nq in range(4):
                    acc.append(psum.tile([P, 512], F32, name="acc%d" % nq, tag="tp"))
            a, b = g // 4, g % 4
            for nq in range(4):
                cols = slice(nq * 512, (nq + 1) * 512)
                nc.tensor.matmul_mx(
                    out=acc[nq][:],
                    lhsT=h_codes[:, g, :].bitcast(FP8X4),
                    lhsT_scale=h_planes[:, g, :],
                    rhs=w2_tiles[g][:, cols].bitcast(FP8X4),
                    rhs_scale=w2_planes[4 * b : P, a, cols],
                    start=(g == 0),
                    stop=(g == G - 1),
                )

        position = SLOTS - 1
        for s in range(1, UNITS + 4):
            if s < UNITS:
                transposes(s)
                copies(s)
            if s >= 4 and s % 2 == 0:
                add_terms((s - 4) // 2)
                relu((s - 4) // 2)
            if s < UNITS:
                edge_column(s)
            if s - 1 < UNITS:
                quantise(s - 1)
            if s >= 5 and s % 2 == 1:
                quantise_h((s - 5) // 2)
            if s >= 3 and s % 2 == 1 and (s - 3) // 2 < G:
                make_addend((s - 3) // 2)
            if 0 <= s - 2 < UNITS:
                layer1(s - 2)
            if s == UNITS:
                layer2(0)
            if s == UNITS + 1:
                layer2(1)
                layer2(2)
            if s == UNITS + 2:
                for half in range(2):
                    b2_bank = psum.tile([P, 1024], BF16, name="b2_bank", tag="tp")
                    for i in range(2):
                        first = 1024 * half + 512 * i
                        nc.tensor.matmul(
                            b2_bank[:, 512 * i : 512 * (i + 1)],
                            lhsT=ones[:],
                            rhs=row[:, first : first + 512],
                            start=True,
                            stop=True,
                        )
                    nc.scalar.copy(out=b2_all[:, 1024 * half : 1024 * (half + 1)], in_=b2_bank[:])
            if position < len(loads):
                issue(loads[position])
                position += 1

        for g in range(3, G):
            layer2(g)
        for nq in range(4):
            cols = slice(nq * 512, (nq + 1) * 512)
            biased = fin.tile([P, 512], F32, name="biased", tag="biased")
            nc.vector.tensor_tensor(out=biased[:], in0=acc[nq][:], in1=b2_all[:, cols], op=ADD)
            result = fin.tile([P, 512], F32, name="result", tag="result")
            nc.scalar.activation(out=result[:], in_=biased[:], func=ACT.Tanh)
            nc.sync.dma_start(out=out[:, cols], in_=result[:])
